import numpy as np
import ml_dtypes


def mxq(x, axis, fmt="e4m3"):
    dtype, down = {"e4m3": (ml_dtypes.float8_e4m3fn, 7), "e5m2": (ml_dtypes.float8_e5m2, 14)}[fmt]
    v = np.moveaxis(np.asarray(x, np.float32).astype(ml_dtypes.bfloat16).astype(np.float64), axis, -1)
    blocks = v.reshape(v.shape[:-1] + (-1, 32))
    amax = np.abs(blocks).max(-1, keepdims=True)
    byte = np.maximum(np.where(amax > 0, np.frexp(amax)[1] - 1 + 127, 0) - down, 1)
    scale = np.exp2(byte - 127.0)
    codes = (blocks / scale).astype(np.float32).astype(dtype).astype(np.float64)
    return np.moveaxis((codes * scale).reshape(v.shape), -1, axis)


WIDE = False


def mx_kscale(k):
    if not WIDE:
        return np.ones(k)
    levels = np.array([10, -10, 5, -5, 0])
    a = np.random.permutation(np.resize(levels, k // 512 * 4)).reshape(k // 512, 4)
    idx = np.arange(k)
    return np.exp2(a[idx // 512, idx % 128 // 32])


BF16 = ml_dtypes.bfloat16


def bf(x):
    return np.asarray(x, np.float32).astype(BF16)


def f64(x):
    return np.asarray(x).astype(np.float64)


B, E, N = 4096, 512, 1024
CLIP_TANH = 10.0
DENS = 0.25


def setup_inputs():
    s, u = mx_kscale(E), mx_kscale(N)
    return {"x": bf(np.random.standard_normal((B, E)) * s),
            "llr": bf(np.random.standard_normal((B, N)) * u),
            "odd_weights": bf(np.random.standard_normal((E, E)) * 1.4 / np.sqrt(DENS * E) / s[:, None]),
            "llr_weights": bf(np.random.standard_normal((N, E)) * 1.4 / np.sqrt(DENS * N) / u[:, None]),
            "w_odd2even_mask": bf((np.random.random((E, E)) < DENS).astype(np.float64)),
            "w_skipconn2even_mask": bf((np.random.random((N, E)) < DENS).astype(np.float64))}


def reference(x, llr, odd_weights, llr_weights, w_odd2even_mask, w_skipconn2even_mask):
    msgs = mxq(f64(x), 1, "e4m3") @ mxq(f64(w_odd2even_mask) * f64(odd_weights), 0, "e4m3")
    skip = mxq(f64(llr), 1, "e4m3") @ mxq(f64(w_skipconn2even_mask) * f64(llr_weights), 0, "e4m3")
    pre = np.clip(msgs + skip, -CLIP_TANH, CLIP_TANH)
    return np.tanh(0.5 * pre)

@@ -1,0 +1,230 @@
+from contextlib import ExitStack
+
+import concourse.mybir as mybir
+from concourse.masks import make_identity
+
+F32 = mybir.dt.float32
+BF16 = mybir.dt.bfloat16
+U32 = mybir.dt.uint32
+U8 = mybir.dt.uint8
+FP8X4 = mybir.dt.float8_e4m3fn_x4
+ALU = mybir.AluOpType
+ACT = mybir.ActivationFunctionType
+
+P = 128
+B, E, N = 4096, 512, 1024
+TILES = B // P
+ROUNDS = TILES // 2
+FLOPS = 2 * B * (E + N) * E
+TANH5 = 0.9999092042625951
+
+UNITS = [(0, 2), (2, 2)] + [(t, 4) for t in range(4, TILES, 4)]
+VB = [32, 32, 84]
+PINNED = True
+
+
+def tile_oddlayer_t_kernel(
+    tc, x, llr, odd_weights, llr_weights, w_odd2even_mask, w_skipconn2even_mask, out
+):
+    nc = tc.nc
+    with ExitStack() as ctx:
+        if PINNED:
+            ctx.enter_context(tc.manual_schedule())
+        const = ctx.enter_context(tc.tile_pool(name="const", bufs=1))
+        acts = ctx.enter_context(tc.tile_pool(name="acts", bufs=1))
+        wpool = ctx.enter_context(tc.tile_pool(name="wpool", bufs=1))
+        gpool = ctx.enter_context(tc.tile_pool(name="gpool", bufs=3))
+        cpool = ctx.enter_context(tc.tile_pool(name="cpool", bufs=4))
+        opool = ctx.enter_context(tc.tile_pool(name="opool", bufs=6))
+        tps = ctx.enter_context(tc.psum_pool(name="tps", bufs=6))
+        ops = ctx.enter_context(tc.psum_pool(name="ops", bufs=2))
+
+        ident = const.tile([P, P], F32)
+        make_identity(nc, ident[:])
+        warm_in = const.tile([P, 1], F32)
+        warm_out = const.tile([P, 1], F32)
+        nc.vector.memset(warm_in[:], 0.0)
+        nc.scalar.activation(out=warm_out[:], in_=warm_in[:], func=ACT.Tanh, scale=0.5)
+
+        w_src = [odd_weights, llr_weights[0:512, :], llr_weights[512:1024, :]]
+        m_src = [w_odd2even_mask, w_skipconn2even_mask[0:512, :], w_skipconn2even_mask[512:1024, :]]
+        wr = []
+        mr = []
+        for g in range(3):
+            wt = wpool.tile([P, 2048], BF16, name="wr%d" % g)
+            mt = wpool.tile([P, 2048], BF16, name="mr%d" % g)
+            for dst, src in ((wt, w_src[g]), (mt, m_src[g])):
+                nc.sync.dma_start(
+                    out=dst[:].rearrange("p (u f) -> p u f", u=2),
+                    in_=src.rearrange("(u p e) c -> p u (e c)", u=2, p=P, e=2),
+                )
+            wr.append(wt)
+            mr.append(mt)
+
+        x_view = x.rearrange("(p t) k -> p (t k)", t=TILES)
+        l_view = llr.rearrange("(p t) k -> p (t k)", t=TILES)
+        o_view = out.rearrange("(p t) e -> p (t e)", t=TILES)
+        where = {}
+        for (t0, n) in UNITS:
+            xs = acts.tile([P, n * E], BF16, name="xs%d" % t0)
+            ls = acts.tile([P, n * N], BF16, name="ls%d" % t0)
+            nc.sync.dma_start(out=xs[:], in_=x_view[:, t0 * E : (t0 + n) * E])
+            nc.sync.dma_start(out=ls[:], in_=l_view[:, t0 * N : (t0 + n) * N])
+            for i in range(n):
+                where[t0 + i] = (xs, ls, i)
+
+        wc = wpool.tile([P, 3 * 512], U32, align_bytes=64)
+        ws = wpool.tile([P, 3 * 512], U8, align_bytes=64)
+        wg = []
+        for g in range(3):
+            wgt = wpool.tile([P, 2048], BF16, name="wg%d" % g, align_bytes=64)
+            wg.append(wgt)
+
+        def w_mult(g):
+            nc.vector.tensor_tensor(out=wr[g][:], in0=wr[g][:], in1=mr[g][:], op=ALU.mult)
+
+        def w_regroup(g):
+            src = wr[g][:].rearrange("p (t c i) -> p c t i", t=4, i=4)
+            dst = wg[g][:].rearrange("p (c i t) -> p c t i", i=4, t=4)
+            nc.vector.tensor_copy(out=dst[:, 0 : VB[g]], in_=src[:, 0 : VB[g]])
+            nc.scalar.copy(out=dst[:, VB[g] : 128], in_=src[:, VB[g] : 128])
+
+        def w_quant(g):
+            nc.vector.quantize_mx(
+                out=wc[:, 512 * g : 512 * g + 512].bitcast(FP8X4),
+                scales=ws[:, 512 * g : 512 * g + 512],
+                in_=wg[g][:],
+            )
+
+        grouped = {}
+        codes = {}
+        obuf = {}
+        pending = []
+
+        def transposes(s, x_on_scalar):
+            gx = gpool.tile([P, 1024], BF16, align_bytes=64)
+            gl = gpool.tile([P, 2048], BF16, align_bytes=64)
+            grouped[s] = (gx, gl)
+            for b in range(3):
+                tp = tps.tile([P, 512], F32)
+                for a in range(2):
+                    for u in range(2):
+                        if b == 0:
+                            xs, ls, i = where[2 * s + a]
+                            src = xs[:].bitcast(F32)[:, i * 256 + 128 * u : i * 256 + 128 * u + 128]
+                        else:
+                            xs, ls, i = where[2 * s + b - 1]
+                            c0 = i * 512 + 256 * a + 128 * u
+                            src = ls[:].bitcast(F32)[:, c0 : c0 + 128]
+                        q = 2 * a + u
+                        nc.tensor.transpose(tp[:, 128 * q : 128 * q + 128], src, ident[:])
+                if b == 0:
+                    dst = gx[:].bitcast(F32)
+                else:
+                    dst = gl[:].bitcast(F32)[:, 512 * (b - 1) : 512 * b]
+                dst = dst.rearrange("p (a r u) -> p a r u", a=2, u=2)
+                srcv = tp[:].rearrange("p (a u r) -> p a r u", a=2, u=2)
+                if b == 0 and not x_on_scalar:
+                    nc.vector.tensor_copy(out=dst, in_=srcv)
+                else:
+                    nc.scalar.copy(out=dst, in_=srcv)
+
+        def quantise(s):
+            gx, gl = grouped[s]
+            cx = cpool.tile([P, 256], U32, align_bytes=64)
+            sx = cpool.tile([P, 256], U8, align_bytes=64)
+            cl = cpool.tile([P, 512], U32, align_bytes=64)
+            sl = cpool.tile([P, 512], U8, align_bytes=64)
+            nc.vector.quantize_mx(out=cx[:].bitcast(FP8X4), scales=sx[:], in_=gx[:])
+            nc.vector.quantize_mx(out=cl[:].bitcast(FP8X4), scales=sl[:], in_=gl[:])
+            codes[s] = (cx, sx, cl, sl)
+
+        def one_pass(acc, s, j, g):
+            cx, sx, cl, sl = codes[s]
+            if g == 0:
+                cc, ss, c0 = cx, sx, 128 * j
+            else:
+                cc, ss, c0 = cl, sl, 256 * j + 128 * (g - 1)
+            nc.tensor.matmul_mx(
+                out=acc[:],
+                lhsT=cc[:, c0 : c0 + 128].bitcast(FP8X4),
+                lhsT_scale=ss[:, c0 : c0 + 128],
+                rhs=wc[:, 512 * g : 512 * g + 512].bitcast(FP8X4),
+                rhs_scale=ws[:, 512 * g : 512 * g + 512],
+                start=(g == 0),
+                stop=(g == 2),
+            )
+
+        def clip(r, j0, j1):
+            ob = obuf[r // 2]
+            c0 = ((2 * r) % 4 + j0) * 512
+            c1 = ((2 * r) % 4 + j1) * 512
+            nc.vector.tensor_scalar(
+                out=ob[:, c0:c1], in0=ob[:, c0:c1], scalar1=TANH5, scalar2=-TANH5,
+                op0=ALU.min, op1=ALU.max,
+            )
+
+        def store(t0, n):
+            ob = obuf[t0 // 4]
+            c0 = (t0 % 4) * 512
+            nc.sync.dma_start(out=o_view[:, t0 * 512 : (t0 + n) * 512], in_=ob[:, c0 : c0 + n * 512])
+
+        def finish(r):
+            if r == ROUNDS - 1:
+                return
+            clip(r, 0, 2)
+            if r == ROUNDS - 2:
+                store(2 * r, 2)
+            elif r % 2 == 1:
+                store(2 * r - 2, 4)
+
+        def matmuls(r, pass_major):
+            if r % 2 == 0:
+                ob = opool.tile([P, 2048], F32)
+                obuf[r // 2] = ob
+            ob = obuf[r // 2]
+            acc0 = ops.tile([P, 512], F32, tag="acc")
+            acc1 = ops.tile([P, 512], F32, tag="acc")
+            accs = [acc0, acc1]
+            if pass_major:
+                order = [(j, g) for g in range(3) for j in range(2)]
+            else:
+                order = [(j, g) for j in range(2) for g in range(3)]
+            for (j, g) in order:
+                one_pass(accs[j], r, j, g)
+            for j in range(2):
+                c0 = ((2 * r) % 4 + j) * 512
+                nc.scalar.activation(out=ob[:, c0 : c0 + 512], in_=accs[j][:], func=ACT.Tanh, scale=0.5)
+                if r == ROUNDS - 1:
+                    clip(r, j, j + 1)
+                    store(2 * r + j, 1)
+
+        w_mult(0)
+        w_regroup(0)
+        w_mult(1)
+        w_quant(0)
+        w_regroup(1)
+        w_mult(2)
+        w_quant(1)
+        w_regroup(2)
+        w_quant(2)
+
+        seq = [("T", 0), ("M", 0), ("T", 1), ("T", 2), ("M", 1), ("T", 3)]
+        for s in range(4, ROUNDS):
+            seq += [("T", s), ("M", s - 2)]
+        seq += [("M", ROUNDS - 2), ("M", ROUNDS - 1)]
+        last_t = max(i for i, ev in enumerate(seq) if ev[0] == "T")
+        for i, (kind, r) in enumerate(seq):
+            if kind == "T":
+                transposes(r, r == 0)
+                for q in pending:
+                    finish(q)
+                pending = []
+                quantise(r)
+            else:
+                if i > last_t:
+                    for q in pending:
+                        finish(q)
+                    pending = []
+                matmuls(r, r == 0)
+                pending.append(r)

@@ -34,8 +34,8 @@ def tile_oddlayer_t_kernel(
         acts = ctx.enter_context(tc.tile_pool(name="acts", bufs=1))
         wpool = ctx.enter_context(tc.tile_pool(name="wpool", bufs=1))
         gpool = ctx.enter_context(tc.tile_pool(name="gpool", bufs=3))
-        cpool = ctx.enter_context(tc.tile_pool(name="cpool", bufs=4))
-        opool = ctx.enter_context(tc.tile_pool(name="opool", bufs=6))
+        cpool = ctx.enter_context(tc.tile_pool(name="cpool", bufs=6))
+        opool = ctx.enter_context(tc.tile_pool(name="opool", bufs=5))
         tps = ctx.enter_context(tc.psum_pool(name="tps", bufs=6))
         ops = ctx.enter_context(tc.psum_pool(name="ops", bufs=2))
 
@@ -209,10 +209,10 @@ def tile_oddlayer_t_kernel(
         w_regroup(2)
         w_quant(2)
 
-        seq = [("T", 0), ("M", 0), ("T", 1), ("T", 2), ("M", 1), ("T", 3)]
-        for s in range(4, ROUNDS):
-            seq += [("T", s), ("M", s - 2)]
-        seq += [("M", ROUNDS - 2), ("M", ROUNDS - 1)]
+        seq = [("T", 0), ("M", 0), ("T", 1), ("T", 2), ("M", 1), ("T", 3), ("T", 4), ("M", 2)]
+        for s in range(5, ROUNDS - 1, 2):
+            seq += [("T", s), ("T", s + 1), ("M", s - 2), ("M", s - 1)]
+        seq += [("T", ROUNDS - 1), ("M", ROUNDS - 3), ("M", ROUNDS - 2), ("M", ROUNDS - 1)]
         last_t = max(i for i, ev in enumerate(seq) if ev[0] == "T")
         for i, (kind, r) in enumerate(seq):
             if kind == "T":

@@ -36,8 +36,8 @@ def tile_oddlayer_t_kernel(
         gpool = ctx.enter_context(tc.tile_pool(name="gpool", bufs=3))
         cpool = ctx.enter_context(tc.tile_pool(name="cpool", bufs=6))
         opool = ctx.enter_context(tc.tile_pool(name="opool", bufs=5))
-        tps = ctx.enter_context(tc.psum_pool(name="tps", bufs=6))
-        ops = ctx.enter_context(tc.psum_pool(name="ops", bufs=2))
+        tps = ctx.enter_context(tc.psum_pool(name="tps", bufs=5))
+        ops = ctx.enter_context(tc.psum_pool(name="ops", bufs=3))
 
         ident = const.tile([P, P], F32)
         make_identity(nc, ident[:])

@@ -18,9 +18,13 @@ ROUNDS = TILES // 2
 FLOPS = 2 * B * (E + N) * E
 TANH5 = 0.9999092042625951
 
-UNITS = [(0, 2), (2, 2)] + [(t, 4) for t in range(4, TILES, 4)]
-VB = [32, 32, 84]
-PINNED = True
+X_UNITS = [(0, 2), (2, 2)] + [(t, 4) for t in range(4, TILES, 4)]
+L_UNITS = [(0, 1), (1, 1)] + [(t, 2) for t in range(2, 12, 2)] + [(t, 4) for t in range(12, TILES, 4)]
+VB = [84, 84, 84]
+HEAD = "c"
+DUMMIES = None
+CLIP_ON_GPSIMD = False
+V_TAKES_L0 = False
 
 
 def tile_oddlayer_t_kernel(
@@ -28,16 +32,15 @@ def tile_oddlayer_t_kernel(
 ):
     nc = tc.nc
     with ExitStack() as ctx:
-        if PINNED:
-            ctx.enter_context(tc.manual_schedule())
+        ctx.enter_context(tc.manual_schedule())
         const = ctx.enter_context(tc.tile_pool(name="const", bufs=1))
         acts = ctx.enter_context(tc.tile_pool(name="acts", bufs=1))
         wpool = ctx.enter_context(tc.tile_pool(name="wpool", bufs=1))
         gpool = ctx.enter_context(tc.tile_pool(name="gpool", bufs=3))
-        cpool = ctx.enter_context(tc.tile_pool(name="cpool", bufs=6))
-        opool = ctx.enter_context(tc.tile_pool(name="opool", bufs=5))
-        tps = ctx.enter_context(tc.psum_pool(name="tps", bufs=5))
-        ops = ctx.enter_context(tc.psum_pool(name="ops", bufs=3))
+        cpool = ctx.enter_context(tc.tile_pool(name="cpool", bufs=4))
+        opool = ctx.enter_context(tc.tile_pool(name="opool", bufs=6))
+        tps = ctx.enter_context(tc.psum_pool(name="tps", bufs=6))
+        ops = ctx.enter_context(tc.psum_pool(name="ops", bufs=2))
 
         ident = const.tile([P, P], F32)
         make_identity(nc, ident[:])
@@ -53,25 +56,32 @@ def tile_oddlayer_t_kernel(
         for g in range(3):
             wt = wpool.tile([P, 2048], BF16, name="wr%d" % g)
             mt = wpool.tile([P, 2048], BF16, name="mr%d" % g)
-            for dst, src in ((wt, w_src[g]), (mt, m_src[g])):
-                nc.sync.dma_start(
-                    out=dst[:].rearrange("p (u f) -> p u f", u=2),
-                    in_=src.rearrange("(u p e) c -> p u (e c)", u=2, p=P, e=2),
-                )
+            for u in range(2):
+                for dst, src in ((wt, w_src[g]), (mt, m_src[g])):
+                    nc.sync.dma_start(
+                        out=dst[:, 1024 * u : 1024 * u + 1024],
+                        in_=src[256 * u : 256 * u + 256, :].rearrange("(p e) c -> p (e c)", e=2),
+                    )
             wr.append(wt)
             mr.append(mt)
 
         x_view = x.rearrange("(p t) k -> p (t k)", t=TILES)
         l_view = llr.rearrange("(p t) k -> p (t k)", t=TILES)
         o_view = out.rearrange("(p t) e -> p (t e)", t=TILES)
-        where = {}
-        for (t0, n) in UNITS:
-            xs = acts.tile([P, n * E], BF16, name="xs%d" % t0)
-            ls = acts.tile([P, n * N], BF16, name="ls%d" % t0)
-            nc.sync.dma_start(out=xs[:], in_=x_view[:, t0 * E : (t0 + n) * E])
-            nc.sync.dma_start(out=ls[:], in_=l_view[:, t0 * N : (t0 + n) * N])
-            for i in range(n):
-                where[t0 + i] = (xs, ls, i)
+        where_x = {}
+        where_l = {}
+        loads = sorted([(t0, 0, n) for (t0, n) in X_UNITS] + [(t0, 1, n) for (t0, n) in L_UNITS])
+        for (t0, kind, n) in loads:
+            if kind == 0:
+                xs = acts.tile([P, n * E], BF16, name="xs%d" % t0)
+                nc.sync.dma_start(out=xs[:], in_=x_view[:, t0 * E : (t0 + n) * E])
+                for i in range(n):
+                    where_x[t0 + i] = (xs, i)
+            else:
+                ls = acts.tile([P, n * N], BF16, name="ls%d" % t0)
+                nc.sync.dma_start(out=ls[:], in_=l_view[:, t0 * N : (t0 + n) * N])
+                for i in range(n):
+                    where_l[t0 + i] = (ls, i)
 
         wc = wpool.tile([P, 3 * 512], U32, align_bytes=64)
         ws = wpool.tile([P, 3 * 512], U8, align_bytes=64)
@@ -80,13 +90,20 @@ def tile_oddlayer_t_kernel(
             wgt = wpool.tile([P, 2048], BF16, name="wg%d" % g, align_bytes=64)
             wg.append(wgt)
 
-        def w_mult(g):
-            nc.vector.tensor_tensor(out=wr[g][:], in0=wr[g][:], in1=mr[g][:], op=ALU.mult)
+        def w_mult(g, u):
+            c0 = 1024 * u
+            nc.vector.tensor_tensor(
+                out=wr[g][:, c0 : c0 + 1024], in0=wr[g][:, c0 : c0 + 1024], in1=mr[g][:, c0 : c0 + 1024], op=ALU.mult
+            )
 
-        def w_regroup(g):
+        def w_regroup_v(g):
             src = wr[g][:].rearrange("p (t c i) -> p c t i", t=4, i=4)
             dst = wg[g][:].rearrange("p (c i t) -> p c t i", i=4, t=4)
             nc.vector.tensor_copy(out=dst[:, 0 : VB[g]], in_=src[:, 0 : VB[g]])
+
+        def w_regroup_s(g):
+            src = wr[g][:].rearrange("p (t c i) -> p c t i", t=4, i=4)
+            dst = wg[g][:].rearrange("p (c i t) -> p c t i", i=4, t=4)
             nc.scalar.copy(out=dst[:, VB[g] : 128], in_=src[:, VB[g] : 128])
 
         def w_quant(g):
@@ -99,48 +116,61 @@ def tile_oddlayer_t_kernel(
         grouped = {}
         codes = {}
         obuf = {}
-        pending = []
+        accs = {}
 
-        def transposes(s, x_on_scalar):
-            gx = gpool.tile([P, 1024], BF16, align_bytes=64)
-            gl = gpool.tile([P, 2048], BF16, align_bytes=64)
-            grouped[s] = (gx, gl)
-            for b in range(3):
-                tp = tps.tile([P, 512], F32)
-                for a in range(2):
-                    for u in range(2):
-                        if b == 0:
-                            xs, ls, i = where[2 * s + a]
-                            src = xs[:].bitcast(F32)[:, i * 256 + 128 * u : i * 256 + 128 * u + 128]
-                        else:
-                            xs, ls, i = where[2 * s + b - 1]
-                            c0 = i * 512 + 256 * a + 128 * u
-                            src = ls[:].bitcast(F32)[:, c0 : c0 + 128]
-                        q = 2 * a + u
-                        nc.tensor.transpose(tp[:, 128 * q : 128 * q + 128], src, ident[:])
-                if b == 0:
-                    dst = gx[:].bitcast(F32)
-                else:
-                    dst = gl[:].bitcast(F32)[:, 512 * (b - 1) : 512 * b]
-                dst = dst.rearrange("p (a r u) -> p a r u", a=2, u=2)
-                srcv = tp[:].rearrange("p (a u r) -> p a r u", a=2, u=2)
-                if b == 0 and not x_on_scalar:
-                    nc.vector.tensor_copy(out=dst, in_=srcv)
-                else:
-                    nc.scalar.copy(out=dst, in_=srcv)
+        def t_bank(s, b, engine):
+            if b == 0:
+                gx = gpool.tile([P, 1024], BF16, align_bytes=64)
+                gl = gpool.tile([P, 2048], BF16, align_bytes=64)
+                grouped[s] = (gx, gl)
+            gx, gl = grouped[s]
+            tp = tps.tile([P, 512], F32)
+            for a in range(2):
+                for u in range(2):
+                    if b == 0:
+                        xs, i = where_x[2 * s + a]
+                        src = xs[:].bitcast(F32)[:, i * 256 + 128 * u : i * 256 + 128 * u + 128]
+                    else:
+                        ls, i = where_l[2 * s + b - 1]
+                        c0 = i * 512 + 256 * a + 128 * u
+                        src = ls[:].bitcast(F32)[:, c0 : c0 + 128]
+                    q = 2 * a + u
+                    nc.tensor.transpose(tp[:, 128 * q : 128 * q + 128], src, ident[:])
+            if b == 0:
+                dst = gx[:].bitcast(F32)
+            else:
+                dst = gl[:].bitcast(F32)[:, 512 * (b - 1) : 512 * b]
+            dst = dst.rearrange("p (a r u) -> p a r u", a=2, u=2)
+            srcv = tp[:].rearrange("p (a u r) -> p a r u", a=2, u=2)
+            if engine == "v":
+                nc.vector.tensor_copy(out=dst, in_=srcv)
+            else:
+                nc.scalar.copy(out=dst, in_=srcv)
 
-        def quantise(s):
+        def q_x(s):
             gx, gl = grouped[s]
             cx = cpool.tile([P, 256], U32, align_bytes=64)
             sx = cpool.tile([P, 256], U8, align_bytes=64)
             cl = cpool.tile([P, 512], U32, align_bytes=64)
             sl = cpool.tile([P, 512], U8, align_bytes=64)
-            nc.vector.quantize_mx(out=cx[:].bitcast(FP8X4), scales=sx[:], in_=gx[:])
-            nc.vector.quantize_mx(out=cl[:].bitcast(FP8X4), scales=sl[:], in_=gl[:])
             codes[s] = (cx, sx, cl, sl)
+            nc.vector.quantize_mx(out=cx[:].bitcast(FP8X4), scales=sx[:], in_=gx[:])
 
-        def one_pass(acc, s, j, g):
+        def q_l(s, j0, j1):
+            gx, gl = grouped[s]
             cx, sx, cl, sl = codes[s]
+            nc.vector.quantize_mx(
+                out=cl[:, 256 * j0 : 256 * j1].bitcast(FP8X4),
+                scales=sl[:, 256 * j0 : 256 * j1],
+                in_=gl[:, 1024 * j0 : 1024 * j1],
+            )
+
+        def one_pass(r, j, g):
+            if g == 0:
+                acc = ops.tile([P, 512], F32)
+                accs[(r, j)] = acc
+            acc = accs[(r, j)]
+            cx, sx, cl, sl = codes[r]
             if g == 0:
                 cc, ss, c0 = cx, sx, 128 * j
             else:
@@ -155,11 +185,19 @@ def tile_oddlayer_t_kernel(
                 stop=(g == 2),
             )
 
-        def clip(r, j0, j1):
+        def tanh(r, j):
+            if r % 2 == 0 and j == 0:
+                ob = opool.tile([P, 2048], F32)
+                obuf[r // 2] = ob
+            ob = obuf[r // 2]
+            c0 = ((2 * r) % 4 + j) * 512
+            nc.scalar.activation(out=ob[:, c0 : c0 + 512], in_=accs[(r, j)][:], func=ACT.Tanh, scale=0.5)
+
+        def clip(r, j0, j1, engine):
             ob = obuf[r // 2]
             c0 = ((2 * r) % 4 + j0) * 512
             c1 = ((2 * r) % 4 + j1) * 512
-            nc.vector.tensor_scalar(
+            engine.tensor_scalar(
                 out=ob[:, c0:c1], in0=ob[:, c0:c1], scalar1=TANH5, scalar2=-TANH5,
                 op0=ALU.min, op1=ALU.max,
             )
@@ -170,61 +208,108 @@ def tile_oddlayer_t_kernel(
             nc.sync.dma_start(out=o_view[:, t0 * 512 : (t0 + n) * 512], in_=ob[:, c0 : c0 + n * 512])
 
         def finish(r):
-            if r == ROUNDS - 1:
-                return
-            clip(r, 0, 2)
-            if r == ROUNDS - 2:
+            if CLIP_ON_GPSIMD and r < ROUNDS - 2:
+                clip(r, 0, 1, nc.gpsimd)
+                clip(r, 1, 2, nc.gpsimd)
+            else:
+                clip(r, 0, 2, nc.vector)
+            if r >= 14:
                 store(2 * r, 2)
             elif r % 2 == 1:
                 store(2 * r - 2, 4)
 
-        def matmuls(r, pass_major):
-            if r % 2 == 0:
-                ob = opool.tile([P, 2048], F32)
-                obuf[r // 2] = ob
-            ob = obuf[r // 2]
-            acc0 = ops.tile([P, 512], F32, tag="acc")
-            acc1 = ops.tile([P, 512], F32, tag="acc")
-            accs = [acc0, acc1]
-            if pass_major:
-                order = [(j, g) for g in range(3) for j in range(2)]
-            else:
-                order = [(j, g) for j in range(2) for g in range(3)]
-            for (j, g) in order:
-                one_pass(accs[j], r, j, g)
+        def dummy(n, src):
+            for i in range(n):
+                junk = ops.tile([P, 512], F32, tag="acc")
+                nc.tensor.matmul(out=junk[:], lhsT=src[:, 0:128], rhs=src[:, 0:512], start=True, stop=True)
+
+        state = {"pending": []}
+
+        def flush():
+            for q in state["pending"]:
+                finish(q)
+            state["pending"] = []
+
+        def transposes(s):
+            t_bank(s, 0, "v")
+            t_bank(s, 1, "v" if (V_TAKES_L0 and s % 2 == 1) else "s")
+            t_bank(s, 2, "s")
+            flush()
+            q_x(s)
+            q_l(s, 0, 2)
+
+        def matmuls(r):
             for j in range(2):
-                c0 = ((2 * r) % 4 + j) * 512
-                nc.scalar.activation(out=ob[:, c0 : c0 + 512], in_=accs[j][:], func=ACT.Tanh, scale=0.5)
+                for g in range(3):
+                    one_pass(r, j, g)
+            for j in range(2):
+                tanh(r, j)
                 if r == ROUNDS - 1:
-                    clip(r, j, j + 1)
+                    clip(r, j, j + 1, nc.vector)
                     store(2 * r + j, 1)
 
-        w_mult(0)
-        w_regroup(0)
-        w_mult(1)
+        w_mult(0, 0)
+        w_mult(0, 1)
+        w_regroup_v(0)
+        w_regroup_s(0)
+        w_mult(1, 0)
         w_quant(0)
-        w_regroup(1)
-        w_mult(2)
+        w_mult(1, 1)
+        w_regroup_v(1)
+        w_regroup_s(1)
+        w_mult(2, 0)
         w_quant(1)
-        w_regroup(2)
+        w_mult(2, 1)
+        w_regroup_v(2)
+        if DUMMIES:
+            dummy(DUMMIES[0], mr[1])
+        if HEAD == "a":
+            w_regroup_s(2)
+            t_bank(0, 0, "s")
+        else:
+            t_bank(0, 0, "s")
+            w_regroup_s(2)
+        if DUMMIES:
+            dummy(DUMMIES[1], mr[1])
+        t_bank(0, 1, "s")
+        if DUMMIES:
+            dummy(DUMMIES[2], mr[1])
+        t_bank(0, 2, "s")
+        if DUMMIES:
+            dummy(DUMMIES[3], mr[1])
+        q_x(0)
         w_quant(2)
+        q_l(0, 0, 1)
+        q_l(0, 1, 2)
+        if HEAD == "c":
+            one_pass(0, 0, 0)
+            one_pass(0, 1, 0)
+            transposes(1)
+            for g in (1, 2):
+                for j in range(2):
+                    one_pass(0, j, g)
+            tanh(0, 0)
+            tanh(0, 1)
+            state["pending"].append(0)
+            seq = [("T", 2), ("M", 1), ("T", 3)]
+        else:
+            for g in range(3):
+                for j in range(2):
+                    one_pass(0, j, g)
+            tanh(0, 0)
+            tanh(0, 1)
+            state["pending"].append(0)
+            seq = [("T", 1), ("T", 2), ("M", 1), ("T", 3)]
 
-        seq = [("T", 0), ("M", 0), ("T", 1), ("T", 2), ("M", 1), ("T", 3), ("T", 4), ("M", 2)]
-        for s in range(5, ROUNDS - 1, 2):
-            seq += [("T", s), ("T", s + 1), ("M", s - 2), ("M", s - 1)]
-        seq += [("T", ROUNDS - 1), ("M", ROUNDS - 3), ("M", ROUNDS - 2), ("M", ROUNDS - 1)]
+        for s in range(4, ROUNDS):
+            seq += [("T", s), ("M", s - 2)]
+        seq += [("M", ROUNDS - 2), ("M", ROUNDS - 1)]
         last_t = max(i for i, ev in enumerate(seq) if ev[0] == "T")
         for i, (kind, r) in enumerate(seq):
             if kind == "T":
-                transposes(r, r == 0)
-                for q in pending:
-                    finish(q)
-                pending = []
-                quantise(r)
+                transposes(r)
             else:
                 if i > last_t:
-                    for q in pending:
-                        finish(q)
-                    pending = []
-                matmuls(r, r == 0)
-                pending.append(r)
+                    flush()
+                matmuls(r)
+                state["pending"].append(r)

@@ -167,7 +167,10 @@ def tile_oddlayer_t_kernel(
 
         def one_pass(r, j, g):
             if g == 0:
-                acc = ops.tile([P, 512], F32)
+                if r >= 13:
+                    acc = tps.tile([P, 512], F32, tag="tp")
+                else:
+                    acc = ops.tile([P, 512], F32)
                 accs[(r, j)] = acc
             acc = accs[(r, j)]
             cx, sx, cl, sl = codes[r]
@@ -213,7 +216,7 @@ def tile_oddlayer_t_kernel(
                 clip(r, 1, 2, nc.gpsimd)
             else:
                 clip(r, 0, 2, nc.vector)
-            if r >= 14:
+            if r >= 10:
                 store(2 * r, 2)
             elif r % 2 == 1:
                 store(2 * r - 2, 4)
@@ -238,13 +241,51 @@ def tile_oddlayer_t_kernel(
             q_x(s)
             q_l(s, 0, 2)
 
+        def last_tile():
+            r, j = ROUNDS - 1, 1
+            cx, sx, cl, sl = codes[r]
+            ob = obuf[r // 2]
+            for h in range(2):
+                half = tps.tile([P, 256], F32, tag="tp")
+                for g in range(3):
+                    if g == 0:
+                        cc, ss, c0 = cx, sx, 128 * j
+                    else:
+                        cc, ss, c0 = cl, sl, 256 * j + 128 * (g - 1)
+                    w0 = 512 * g + 256 * h
+                    nc.tensor.matmul_mx(
+                        out=half[:],
+                        lhsT=cc[:, c0 : c0 + 128].bitcast(FP8X4),
+                        lhsT_scale=ss[:, c0 : c0 + 128],
+                        rhs=wc[:, w0 : w0 + 256].bitcast(FP8X4),
+                        rhs_scale=ws[:, w0 : w0 + 256],
+                        start=(g == 0),
+                        stop=(g == 2),
+                    )
+                o0 = 3 * 512 + 256 * h
+                seg = ob[:, o0 : o0 + 256]
+                nc.scalar.activation(out=seg, in_=half[:], func=ACT.Tanh, scale=0.5)
+                nc.vector.tensor_scalar(
+                    out=seg, in0=seg, scalar1=TANH5, scalar2=-TANH5, op0=ALU.min, op1=ALU.max
+                )
+                d0 = (TILES - 1) * 512 + 256 * h
+                nc.sync.dma_start(out=o_view[:, d0 : d0 + 256], in_=seg)
+
         def matmuls(r):
+            if r == ROUNDS - 1:
+                for g in range(3):
+                    one_pass(r, 0, g)
+                tanh(r, 0)
+                clip(r, 0, 1, nc.vector)
+                store(2 * r, 1)
+                last_tile()
+                return
             for j in range(2):
                 for g in range(3):
                     one_pass(r, j, g)
             for j in range(2):
                 tanh(r, j)
-                if r == ROUNDS - 1:
+                if r >= 13:
                     clip(r, j, j + 1, nc.vector)
                     store(2 * r + j, 1)
 
@@ -312,4 +353,5 @@ def tile_oddlayer_t_kernel(
                 if i > last_t:
                     flush()
                 matmuls(r)
-                state["pending"].append(r)
+                if r < 13:
+                    state["pending"].append(r)

@@ -342,16 +342,20 @@ def tile_oddlayer_t_kernel(
             state["pending"].append(0)
             seq = [("T", 1), ("T", 2), ("M", 1), ("T", 3)]
 
-        for s in range(4, ROUNDS):
-            seq += [("T", s), ("M", s - 2)]
-        seq += [("M", ROUNDS - 2), ("M", ROUNDS - 1)]
-        last_t = max(i for i, ev in enumerate(seq) if ev[0] == "T")
-        for i, (kind, r) in enumerate(seq):
-            if kind == "T":
-                transposes(r)
-            else:
-                if i > last_t:
+        banks = [(s, b) for s in range(2, ROUNDS) for b in range(3)]
+        for r in range(1, ROUNDS):
+            n = ([4,4,4] + [3] * ROUNDS)[r - 1]
+            run = banks[:n]
+            banks = banks[n:]
+            for i, (s, b) in enumerate(run):
+                t_bank(s, b, "v" if b == 0 else "s")
+                if i == 0:
                     flush()
-                matmuls(r)
-                if r < 13:
-                    state["pending"].append(r)
+                if b == 2:
+                    q_x(s)
+                    q_l(s, 0, 2)
+            if not run:
+                flush()
+            matmuls(r)
+            if r < 13:
+                state["pending"].append(r)

@@ -221,10 +221,13 @@ def tile_oddlayer_t_kernel(
             elif r % 2 == 1:
                 store(2 * r - 2, 4)
 
-        def dummy(n, src):
+        def dummy(n, g, u):
+            c0 = 1024 * u
             for i in range(n):
                 junk = ops.tile([P, 512], F32, tag="acc")
-                nc.tensor.matmul(out=junk[:], lhsT=src[:, 0:128], rhs=src[:, 0:512], start=True, stop=True)
+                nc.tensor.matmul(
+                    out=junk[:], lhsT=mr[g][:, c0 : c0 + 128], rhs=mr[g][:, c0 : c0 + 512], start=True, stop=True
+                )
 
         state = {"pending": []}
 
@@ -302,22 +305,20 @@ def tile_oddlayer_t_kernel(
         w_quant(1)
         w_mult(2, 1)
         w_regroup_v(2)
-        if DUMMIES:
-            dummy(DUMMIES[0], mr[1])
+        dummy(5, 1, 0)
+        dummy(4, 2, 0)
+        dummy(2, 2, 1)
         if HEAD == "a":
             w_regroup_s(2)
             t_bank(0, 0, "s")
         else:
             t_bank(0, 0, "s")
             w_regroup_s(2)
-        if DUMMIES:
-            dummy(DUMMIES[1], mr[1])
+        dummy(1, 2, 1)
         t_bank(0, 1, "s")
-        if DUMMIES:
-            dummy(DUMMIES[2], mr[1])
+        dummy(1, 2, 1)
         t_bank(0, 2, "s")
-        if DUMMIES:
-            dummy(DUMMIES[3], mr[1])
+        dummy(1, 2, 1)
         q_x(0)
         w_quant(2)
         q_l(0, 0, 1)
@@ -344,7 +345,7 @@ def tile_oddlayer_t_kernel(
 
         banks = [(s, b) for s in range(2, ROUNDS) for b in range(3)]
         for r in range(1, ROUNDS):
-            n = ([4,4,4] + [3] * ROUNDS)[r - 1]
+            n = ([3,6] + [3] * ROUNDS)[r - 1]
             run = banks[:n]
             banks = banks[n:]
             for i, (s, b) in enumerate(run):

@@ -14,17 +14,17 @@ ACT = mybir.ActivationFunctionType
 P = 128
 B, E, N = 4096, 512, 1024
 TILES = B // P
-ROUNDS = TILES // 2
+PAIRS = TILES // 2
 FLOPS = 2 * B * (E + N) * E
 TANH5 = 0.9999092042625951
 
-X_UNITS = [(0, 2), (2, 2)] + [(t, 4) for t in range(4, TILES, 4)]
-L_UNITS = [(0, 1), (1, 1)] + [(t, 2) for t in range(2, 12, 2)] + [(t, 4) for t in range(12, TILES, 4)]
-VB = [84, 84, 84]
-HEAD = "c"
-DUMMIES = None
-CLIP_ON_GPSIMD = False
-V_TAKES_L0 = False
+LOADS = (
+    [("w", 0), ("x", 0, 2), ("x", 2, 4), ("w", 1), ("l", 0, 2), ("w", 2), ("l", 2, 2), ("l", 4, 2), ("x", 6, 2), ("l", 6, 2)]
+    + [(k, t + i, n) for t in (8, 12) for (k, i, n) in (("x", 0, 4), ("l", 0, 2), ("l", 2, 2))]
+    + [(k, t, 4) for t in range(16, TILES, 4) for k in ("x", "l")]
+)
+VC = 192
+GROUPS = [[3], [4], [5], [6], [7], [8], [9], [10], [11], [12], [13], [14], [15]]
 
 
 def tile_oddlayer_t_kernel(
@@ -37,10 +37,9 @@ def tile_oddlayer_t_kernel(
         acts = ctx.enter_context(tc.tile_pool(name="acts", bufs=1))
         wpool = ctx.enter_context(tc.tile_pool(name="wpool", bufs=1))
         gpool = ctx.enter_context(tc.tile_pool(name="gpool", bufs=3))
-        cpool = ctx.enter_context(tc.tile_pool(name="cpool", bufs=4))
+        cpool = ctx.enter_context(tc.tile_pool(name="cpool", bufs=5))
         opool = ctx.enter_context(tc.tile_pool(name="opool", bufs=6))
-        tps = ctx.enter_context(tc.psum_pool(name="tps", bufs=6))
-        ops = ctx.enter_context(tc.psum_pool(name="ops", bufs=2))
+        psum = ctx.enter_context(tc.psum_pool(name="psum", bufs=1))
 
         ident = const.tile([P, P], F32)
         make_identity(nc, ident[:])
@@ -51,33 +50,34 @@ def tile_oddlayer_t_kernel(
 
         w_src = [odd_weights, llr_weights[0:512, :], llr_weights[512:1024, :]]
         m_src = [w_odd2even_mask, w_skipconn2even_mask[0:512, :], w_skipconn2even_mask[512:1024, :]]
-        wr = []
-        mr = []
-        for g in range(3):
-            wt = wpool.tile([P, 2048], BF16, name="wr%d" % g)
-            mt = wpool.tile([P, 2048], BF16, name="mr%d" % g)
-            for u in range(2):
-                for dst, src in ((wt, w_src[g]), (mt, m_src[g])):
-                    nc.sync.dma_start(
-                        out=dst[:, 1024 * u : 1024 * u + 1024],
-                        in_=src[256 * u : 256 * u + 256, :].rearrange("(p e) c -> p (e c)", e=2),
-                    )
-            wr.append(wt)
-            mr.append(mt)
-
         x_view = x.rearrange("(p t) k -> p (t k)", t=TILES)
         l_view = llr.rearrange("(p t) k -> p (t k)", t=TILES)
         o_view = out.rearrange("(p t) e -> p (t e)", t=TILES)
+        wr = {}
+        mr = {}
         where_x = {}
         where_l = {}
-        loads = sorted([(t0, 0, n) for (t0, n) in X_UNITS] + [(t0, 1, n) for (t0, n) in L_UNITS])
-        for (t0, kind, n) in loads:
-            if kind == 0:
+        for load in LOADS:
+            if load[0] == "w":
+                g = load[1]
+                wt = wpool.tile([P, 2048], BF16, name="wr%d" % g)
+                mt = wpool.tile([P, 2048], BF16, name="mr%d" % g)
+                for u in range(2):
+                    for dst, src in ((wt, w_src[g]), (mt, m_src[g])):
+                        nc.sync.dma_start(
+                            out=dst[:, 1024 * u : 1024 * u + 1024],
+                            in_=src[256 * u : 256 * u + 256, :].rearrange("(p e) c -> p (e c)", e=2),
+                        )
+                wr[g] = wt
+                mr[g] = mt
+            elif load[0] == "x":
+                t0, n = load[1], load[2]
                 xs = acts.tile([P, n * E], BF16, name="xs%d" % t0)
                 nc.sync.dma_start(out=xs[:], in_=x_view[:, t0 * E : (t0 + n) * E])
                 for i in range(n):
                     where_x[t0 + i] = (xs, i)
             else:
+                t0, n = load[1], load[2]
                 ls = acts.tile([P, n * N], BF16, name="ls%d" % t0)
                 nc.sync.dma_start(out=ls[:], in_=l_view[:, t0 * N : (t0 + n) * N])
                 for i in range(n):
@@ -90,21 +90,24 @@ def tile_oddlayer_t_kernel(
             wgt = wpool.tile([P, 2048], BF16, name="wg%d" % g, align_bytes=64)
             wg.append(wgt)
 
-        def w_mult(g, u):
-            c0 = 1024 * u
-            nc.vector.tensor_tensor(
-                out=wr[g][:, c0 : c0 + 1024], in0=wr[g][:, c0 : c0 + 1024], in1=mr[g][:, c0 : c0 + 1024], op=ALU.mult
-            )
-
-        def w_regroup_v(g):
-            src = wr[g][:].rearrange("p (t c i) -> p c t i", t=4, i=4)
-            dst = wg[g][:].rearrange("p (c i t) -> p c t i", i=4, t=4)
-            nc.vector.tensor_copy(out=dst[:, 0 : VB[g]], in_=src[:, 0 : VB[g]])
+        def w_mask(g, u):
+            half = slice(1024 * u, 1024 * u + 1024)
+            w3 = wr[g][:, half].rearrange("p (e c) -> p e c", e=2)[:, :, VC:512]
+            m3 = mr[g][:, half].rearrange("p (e c) -> p e c", e=2)[:, :, VC:512]
+            nc.vector.tensor_tensor(out=w3, in0=w3, in1=m3, op=ALU.mult)
 
         def w_regroup_s(g):
             src = wr[g][:].rearrange("p (t c i) -> p c t i", t=4, i=4)
             dst = wg[g][:].rearrange("p (c i t) -> p c t i", i=4, t=4)
-            nc.scalar.copy(out=dst[:, VB[g] : 128], in_=src[:, VB[g] : 128])
+            nc.scalar.copy(out=dst[:, VC // 4 : 128], in_=src[:, VC // 4 : 128])
+
+        def w_fused_v(g):
+            nc.vector.tensor_tensor(
+                out=wg[g][:, 0 : 4 * VC].rearrange("p (c t) -> p c t", t=4),
+                in0=wr[g][:].rearrange("p (t c) -> p c t", t=4)[:, 0:VC],
+                in1=mr[g][:].rearrange("p (t c) -> p c t", t=4)[:, 0:VC],
+                op=ALU.mult,
+            )
 
         def w_quant(g):
             nc.vector.quantize_mx(
@@ -112,6 +115,13 @@ def tile_oddlayer_t_kernel(
                 scales=ws[:, 512 * g : 512 * g + 512],
                 in_=wg[g][:],
             )
+
+        free = list(range(8))
+
+        def take():
+            k = free[0]
+            free.remove(k)
+            return k
 
         grouped = {}
         codes = {}
@@ -124,7 +134,8 @@ def tile_oddlayer_t_kernel(
                 gl = gpool.tile([P, 2048], BF16, align_bytes=64)
                 grouped[s] = (gx, gl)
             gx, gl = grouped[s]
-            tp = tps.tile([P, 512], F32)
+            k = take()
+            tp = psum.tile([P, 512], F32, tag="bank%d" % k)
             for a in range(2):
                 for u in range(2):
                     if b == 0:
@@ -146,6 +157,7 @@ def tile_oddlayer_t_kernel(
                 nc.vector.tensor_copy(out=dst, in_=srcv)
             else:
                 nc.scalar.copy(out=dst, in_=srcv)
+            free.append(k)
 
         def q_x(s):
             gx, gl = grouped[s]
@@ -167,12 +179,10 @@ def tile_oddlayer_t_kernel(
 
         def one_pass(r, j, g):
             if g == 0:
-                if r >= 13:
-                    acc = tps.tile([P, 512], F32, tag="tp")
-                else:
-                    acc = ops.tile([P, 512], F32)
-                accs[(r, j)] = acc
-            acc = accs[(r, j)]
+                k = take()
+                acc = psum.tile([P, 512], F32, tag="bank%d" % k)
+                accs[(r, j)] = (acc, k)
+            acc, k = accs[(r, j)]
             cx, sx, cl, sl = codes[r]
             if g == 0:
                 cc, ss, c0 = cx, sx, 128 * j
@@ -194,13 +204,15 @@ def tile_oddlayer_t_kernel(
                 obuf[r // 2] = ob
             ob = obuf[r // 2]
             c0 = ((2 * r) % 4 + j) * 512
-            nc.scalar.activation(out=ob[:, c0 : c0 + 512], in_=accs[(r, j)][:], func=ACT.Tanh, scale=0.5)
+            acc, k = accs[(r, j)]
+            nc.scalar.activation(out=ob[:, c0 : c0 + 512], in_=acc[:], func=ACT.Tanh, scale=0.5)
+            free.append(k)
 
-        def clip(r, j0, j1, engine):
+        def clip(r, j0, j1):
             ob = obuf[r // 2]
             c0 = ((2 * r) % 4 + j0) * 512
             c1 = ((2 * r) % 4 + j1) * 512
-            engine.tensor_scalar(
+            nc.vector.tensor_scalar(
                 out=ob[:, c0:c1], in0=ob[:, c0:c1], scalar1=TANH5, scalar2=-TANH5,
                 op0=ALU.min, op1=ALU.max,
             )
@@ -210,46 +222,34 @@ def tile_oddlayer_t_kernel(
             c0 = (t0 % 4) * 512
             nc.sync.dma_start(out=o_view[:, t0 * 512 : (t0 + n) * 512], in_=ob[:, c0 : c0 + n * 512])
 
-        def finish(r):
-            if CLIP_ON_GPSIMD and r < ROUNDS - 2:
-                clip(r, 0, 1, nc.gpsimd)
-                clip(r, 1, 2, nc.gpsimd)
-            else:
-                clip(r, 0, 2, nc.vector)
-            if r >= 10:
-                store(2 * r, 2)
-            elif r % 2 == 1:
-                store(2 * r - 2, 4)
+        pending = []
+
+        def flush():
+            for r in pending:
+                clip(r, 0, 2)
+                if r >= 10:
+                    store(2 * r, 2)
+                elif r % 2 == 1:
+                    store(2 * r - 2, 4)
+            pending.clear()
 
         def dummy(n, g, u):
             c0 = 1024 * u
             for i in range(n):
-                junk = ops.tile([P, 512], F32, tag="acc")
+                k = take()
+                junk = psum.tile([P, 512], F32, tag="bank%d" % k)
                 nc.tensor.matmul(
                     out=junk[:], lhsT=mr[g][:, c0 : c0 + 128], rhs=mr[g][:, c0 : c0 + 512], start=True, stop=True
                 )
-
-        state = {"pending": []}
-
-        def flush():
-            for q in state["pending"]:
-                finish(q)
-            state["pending"] = []
-
-        def transposes(s):
-            t_bank(s, 0, "v")
-            t_bank(s, 1, "v" if (V_TAKES_L0 and s % 2 == 1) else "s")
-            t_bank(s, 2, "s")
-            flush()
-            q_x(s)
-            q_l(s, 0, 2)
+                free.append(k)
 
         def last_tile():
-            r, j = ROUNDS - 1, 1
+            r, j = PAIRS - 1, 1
             cx, sx, cl, sl = codes[r]
             ob = obuf[r // 2]
             for h in range(2):
-                half = tps.tile([P, 256], F32, tag="tp")
+                k = take()
+                half = psum.tile([P, 256], F32, tag="bank%d" % k)
                 for g in range(3):
                     if g == 0:
                         cc, ss, c0 = cx, sx, 128 * j
@@ -274,89 +274,85 @@ def tile_oddlayer_t_kernel(
                 d0 = (TILES - 1) * 512 + 256 * h
                 nc.sync.dma_start(out=o_view[:, d0 : d0 + 256], in_=seg)
 
-        def matmuls(r):
-            if r == ROUNDS - 1:
-                for g in range(3):
-                    one_pass(r, 0, g)
-                tanh(r, 0)
-                clip(r, 0, 1, nc.vector)
-                store(2 * r, 1)
-                last_tile()
-                return
-            for j in range(2):
-                for g in range(3):
-                    one_pass(r, j, g)
-            for j in range(2):
-                tanh(r, j)
-                if r >= 13:
-                    clip(r, j, j + 1, nc.vector)
-                    store(2 * r + j, 1)
-
-        w_mult(0, 0)
-        w_mult(0, 1)
-        w_regroup_v(0)
+        w_mask(0, 0)
+        w_mask(0, 1)
         w_regroup_s(0)
-        w_mult(1, 0)
+        w_fused_v(0)
+        dummy(5, 0, 0)
+        t_bank(0, 0, "v")
+        t_bank(1, 0, "s")
         w_quant(0)
-        w_mult(1, 1)
-        w_regroup_v(1)
-        w_regroup_s(1)
-        w_mult(2, 0)
-        w_quant(1)
-        w_mult(2, 1)
-        w_regroup_v(2)
-        dummy(5, 1, 0)
-        dummy(4, 2, 0)
-        dummy(2, 2, 1)
-        if HEAD == "a":
-            w_regroup_s(2)
-            t_bank(0, 0, "s")
-        else:
-            t_bank(0, 0, "s")
-            w_regroup_s(2)
-        dummy(1, 2, 1)
-        t_bank(0, 1, "s")
-        dummy(1, 2, 1)
-        t_bank(0, 2, "s")
-        dummy(1, 2, 1)
+        t_bank(2, 0, "s")
+        dummy(2, 0, 1)
         q_x(0)
-        w_quant(2)
+        q_x(1)
+        w_mask(1, 0)
+        q_x(2)
+        for r in range(3):
+            for j in range(2):
+                one_pass(r, j, 0)
+        w_mask(1, 1)
+        w_regroup_s(1)
+        w_fused_v(1)
+        t_bank(0, 1, "v")
+        w_quant(1)
+        t_bank(0, 2, "s")
+        dummy(2, 1, 0)
         q_l(0, 0, 1)
         q_l(0, 1, 2)
-        if HEAD == "c":
-            one_pass(0, 0, 0)
-            one_pass(0, 1, 0)
-            transposes(1)
-            for g in (1, 2):
-                for j in range(2):
-                    one_pass(0, j, g)
-            tanh(0, 0)
-            tanh(0, 1)
-            state["pending"].append(0)
-            seq = [("T", 2), ("M", 1), ("T", 3)]
-        else:
-            for g in range(3):
-                for j in range(2):
-                    one_pass(0, j, g)
-            tanh(0, 0)
-            tanh(0, 1)
-            state["pending"].append(0)
-            seq = [("T", 1), ("T", 2), ("M", 1), ("T", 3)]
+        one_pass(0, 0, 1)
+        one_pass(0, 1, 1)
+        w_mask(2, 0)
+        w_mask(2, 1)
+        w_regroup_s(2)
+        w_fused_v(2)
+        t_bank(1, 1, "v")
+        w_quant(2)
+        t_bank(1, 2, "s")
+        q_l(1, 0, 2)
+        t_bank(2, 1, "s")
+        t_bank(2, 2, "s")
+        for j in range(2):
+            one_pass(0, j, 2)
+            tanh(0, j)
+        q_l(2, 0, 2)
+        pending.append(0)
+        queue = [[1], [2]] + GROUPS
 
-        banks = [(s, b) for s in range(2, ROUNDS) for b in range(3)]
-        for r in range(1, ROUNDS):
-            n = ([3,6] + [3] * ROUNDS)[r - 1]
-            run = banks[:n]
-            banks = banks[n:]
-            for i, (s, b) in enumerate(run):
-                t_bank(s, b, "v" if b == 0 else "s")
+        def transposes(group):
+            for i, s in enumerate(group):
+                t_bank(s, 0, "v")
                 if i == 0:
                     flush()
-                if b == 2:
-                    q_x(s)
-                    q_l(s, 0, 2)
-            if not run:
+                t_bank(s, 1, "s")
+                t_bank(s, 2, "s")
+                q_x(s)
+                q_l(s, 0, 2)
+
+        def matmuls(group):
+            for r in group:
+                first = 1 if r in (1, 2) else 0
+                if r == PAIRS - 1:
+                    for g in range(3):
+                        one_pass(r, 0, g)
+                    tanh(r, 0)
+                    clip(r, 0, 1)
+                    store(2 * r, 1)
+                    last_tile()
+                    continue
+                for j in range(2):
+                    for g in range(first, 3):
+                        one_pass(r, j, g)
+                    tanh(r, j)
+                    if r >= 13:
+                        clip(r, j, j + 1)
+                        store(2 * r + j, 1)
+                if r < 13:
+                    pending.append(r)
+
+        for i, group in enumerate(queue):
+            if i + 2 < len(queue):
+                transposes(queue[i + 2])
+            else:
                 flush()
-            matmuls(r)
-            if r < 13:
-                state["pending"].append(r)
+            matmuls(group)

@@ -23,8 +23,10 @@ LOADS = (
     + [(k, t + i, n) for t in (8, 12) for (k, i, n) in (("x", 0, 4), ("l", 0, 2), ("l", 2, 2))]
     + [(k, t, 4) for t in range(16, TILES, 4) for k in ("x", "l")]
 )
-VC = 192
-GROUPS = [[3], [4], [5], [6], [7], [8], [9], [10], [11], [12], [13], [14], [15]]
+VC = [320, 256, 288]
+RUN_BANKS = 3
+RUN_PASSES = 6
+FIRST_BANKS = 6
 
 
 def tile_oddlayer_t_kernel(
@@ -92,20 +94,20 @@ def tile_oddlayer_t_kernel(
 
         def w_mask(g, u):
             half = slice(1024 * u, 1024 * u + 1024)
-            w3 = wr[g][:, half].rearrange("p (e c) -> p e c", e=2)[:, :, VC:512]
-            m3 = mr[g][:, half].rearrange("p (e c) -> p e c", e=2)[:, :, VC:512]
+            w3 = wr[g][:, half].rearrange("p (e c) -> p e c", e=2)[:, :, VC[g] : 512]
+            m3 = mr[g][:, half].rearrange("p (e c) -> p e c", e=2)[:, :, VC[g] : 512]
             nc.vector.tensor_tensor(out=w3, in0=w3, in1=m3, op=ALU.mult)
 
         def w_regroup_s(g):
             src = wr[g][:].rearrange("p (t c i) -> p c t i", t=4, i=4)
             dst = wg[g][:].rearrange("p (c i t) -> p c t i", i=4, t=4)
-            nc.scalar.copy(out=dst[:, VC // 4 : 128], in_=src[:, VC // 4 : 128])
+            nc.scalar.copy(out=dst[:, VC[g] // 4 : 128], in_=src[:, VC[g] // 4 : 128])
 
         def w_fused_v(g):
             nc.vector.tensor_tensor(
-                out=wg[g][:, 0 : 4 * VC].rearrange("p (c t) -> p c t", t=4),
-                in0=wr[g][:].rearrange("p (t c) -> p c t", t=4)[:, 0:VC],
-                in1=mr[g][:].rearrange("p (t c) -> p c t", t=4)[:, 0:VC],
+                out=wg[g][:, 0 : 4 * VC[g]].rearrange("p (c t) -> p c t", t=4),
+                in0=wr[g][:].rearrange("p (t c) -> p c t", t=4)[:, 0 : VC[g]],
+                in1=mr[g][:].rearrange("p (t c) -> p c t", t=4)[:, 0 : VC[g]],
                 op=ALU.mult,
             )
 
@@ -236,12 +238,10 @@ def tile_oddlayer_t_kernel(
         def dummy(n, g, u):
             c0 = 1024 * u
             for i in range(n):
-                k = take()
-                junk = psum.tile([P, 512], F32, tag="bank%d" % k)
+                junk = psum.tile([P, 512], F32, tag="bank%d" % free[0])
                 nc.tensor.matmul(
                     out=junk[:], lhsT=mr[g][:, c0 : c0 + 128], rhs=mr[g][:, c0 : c0 + 512], start=True, stop=True
                 )
-                free.append(k)
 
         def last_tile():
             r, j = PAIRS - 1, 1
@@ -278,81 +278,83 @@ def tile_oddlayer_t_kernel(
         w_mask(0, 1)
         w_regroup_s(0)
         w_fused_v(0)
-        dummy(5, 0, 0)
-        t_bank(0, 0, "v")
+        dummy(3, 0, 0)
+        t_bank(0, 0, "s")
         t_bank(1, 0, "s")
-        w_quant(0)
         t_bank(2, 0, "s")
-        dummy(2, 0, 1)
+        dummy(1, 0, 0)
+        w_quant(0)
         q_x(0)
-        q_x(1)
         w_mask(1, 0)
-        q_x(2)
-        for r in range(3):
+        q_x(1)
+        for r in range(2):
             for j in range(2):
                 one_pass(r, j, 0)
+        dummy(1, 0, 0)
         w_mask(1, 1)
         w_regroup_s(1)
         w_fused_v(1)
-        t_bank(0, 1, "v")
-        w_quant(1)
+        t_bank(0, 1, "s")
         t_bank(0, 2, "s")
-        dummy(2, 1, 0)
+        q_x(2)
+        w_quant(1)
+        w_mask(2, 0)
         q_l(0, 0, 1)
         q_l(0, 1, 2)
-        one_pass(0, 0, 1)
-        one_pass(0, 1, 1)
-        w_mask(2, 0)
         w_mask(2, 1)
         w_regroup_s(2)
         w_fused_v(2)
-        t_bank(1, 1, "v")
-        w_quant(2)
+        dummy(5, 0, 0)
+        one_pass(0, 0, 1)
+        one_pass(0, 1, 1)
+        t_bank(1, 1, "s")
         t_bank(1, 2, "s")
-        q_l(1, 0, 2)
-        t_bank(2, 1, "s")
+        w_quant(2)
+        t_bank(2, 1, "v")
         t_bank(2, 2, "s")
+        q_l(1, 0, 1)
+        q_l(1, 1, 2)
+        dummy(2, 0, 0)
         for j in range(2):
             one_pass(0, j, 2)
             tanh(0, j)
-        q_l(2, 0, 2)
-        pending.append(0)
-        queue = [[1], [2]] + GROUPS
+        q_l(2, 0, 1)
+        for j in range(2):
+            one_pass(1, j, 1)
+            one_pass(1, j, 2)
+            tanh(1, j)
+        q_l(2, 1, 2)
+        pending.extend([0, 1])
 
-        def transposes(group):
-            for i, s in enumerate(group):
-                t_bank(s, 0, "v")
+
+        banks = [(s, b) for s in range(3, PAIRS) for b in range(3)]
+        passes = [(r, j, g) for r in range(2, PAIRS) for j in range(2) for g in range(3)]
+        passes = passes[:-3]
+        first = True
+        while passes:
+            n = FIRST_BANKS if first else RUN_BANKS
+            first = False
+            run = banks[:n]
+            banks = banks[n:]
+            for i, (s, b) in enumerate(run):
+                t_bank(s, b, "v" if b == 0 else "s")
                 if i == 0:
                     flush()
-                t_bank(s, 1, "s")
-                t_bank(s, 2, "s")
-                q_x(s)
-                q_l(s, 0, 2)
-
-        def matmuls(group):
-            for r in group:
-                first = 1 if r in (1, 2) else 0
-                if r == PAIRS - 1:
-                    for g in range(3):
-                        one_pass(r, 0, g)
-                    tanh(r, 0)
-                    clip(r, 0, 1)
-                    store(2 * r, 1)
-                    last_tile()
-                    continue
-                for j in range(2):
-                    for g in range(first, 3):
-                        one_pass(r, j, g)
+                if b == 1:
+                    q_x(s)
+                if b == 2:
+                    q_l(s, 0, 2)
+            if not run:
+                flush()
+            part = passes[:RUN_PASSES]
+            passes = passes[RUN_PASSES:]
+            for (r, j, g) in part:
+                one_pass(r, j, g)
+                if g == 2:
                     tanh(r, j)
                     if r >= 13:
                         clip(r, j, j + 1)
                         store(2 * r + j, 1)
-                if r < 13:
-                    pending.append(r)
-
-        for i, group in enumerate(queue):
-            if i + 2 < len(queue):
-                transposes(queue[i + 2])
-            else:
-                flush()
-            matmuls(group)
+                    elif j == 1:
+                        pending.append(r)
+        last_tile()

@@ -24,9 +24,9 @@ LOADS = (
     + [(k, t, 4) for t in range(16, TILES, 4) for k in ("x", "l")]
 )
 VC = [320, 256, 288]
-RUN_BANKS = 3
-RUN_PASSES = 6
-FIRST_BANKS = 6
+RUN_BANKS = 4
+RUN_PASSES = 8
+FIRST_BANKS = 5
 
 
 def tile_oddlayer_t_kernel(
@@ -237,14 +237,14 @@ def tile_oddlayer_t_kernel(
 
         def dummy(n, g, u):
             c0 = 1024 * u
+            junk = psum.tile([P, 512], F32, tag="bank%d" % free[1])
             for i in range(n):
-                junk = psum.tile([P, 512], F32, tag="bank%d" % free[0])
                 nc.tensor.matmul(
-                    out=junk[:], lhsT=mr[g][:, c0 : c0 + 128], rhs=mr[g][:, c0 : c0 + 512], start=True, stop=True
+                    out=junk[:], lhsT=mr[g][:, c0 : c0 + 128], rhs=mr[g][:, c0 : c0 + 512],
+                    start=(i == 0), stop=(i == n - 1),
                 )
 
-        def last_tile():
-            r, j = PAIRS - 1, 1
+        def by_halves(r, j):
             cx, sx, cl, sl = codes[r]
             ob = obuf[r // 2]
             for h in range(2):
@@ -265,13 +265,13 @@ def tile_oddlayer_t_kernel(
                         start=(g == 0),
                         stop=(g == 2),
                     )
-                o0 = 3 * 512 + 256 * h
+                o0 = ((2 * r) % 4 + j) * 512 + 256 * h
                 seg = ob[:, o0 : o0 + 256]
                 nc.scalar.activation(out=seg, in_=half[:], func=ACT.Tanh, scale=0.5)
                 nc.vector.tensor_scalar(
                     out=seg, in0=seg, scalar1=TANH5, scalar2=-TANH5, op0=ALU.min, op1=ALU.max
                 )
-                d0 = (TILES - 1) * 512 + 256 * h
+                d0 = (2 * r + j) * 512 + 256 * h
                 nc.sync.dma_start(out=o_view[:, d0 : d0 + 256], in_=seg)
 
         w_mask(0, 0)
@@ -280,6 +280,7 @@ def tile_oddlayer_t_kernel(
         w_fused_v(0)
         dummy(3, 0, 0)
         t_bank(0, 0, "s")
+        dummy(1, 0, 0)
         t_bank(1, 0, "s")
         t_bank(2, 0, "s")
         dummy(1, 0, 0)
@@ -304,17 +305,16 @@ def tile_oddlayer_t_kernel(
         w_mask(2, 1)
         w_regroup_s(2)
         w_fused_v(2)
-        dummy(5, 0, 0)
+        dummy(8, 0, 0)
         one_pass(0, 0, 1)
         one_pass(0, 1, 1)
         t_bank(1, 1, "s")
         t_bank(1, 2, "s")
         w_quant(2)
-        t_bank(2, 1, "v")
+        t_bank(2, 1, "s")
         t_bank(2, 2, "s")
         q_l(1, 0, 1)
         q_l(1, 1, 2)
-        dummy(2, 0, 0)
         for j in range(2):
             one_pass(0, j, 2)
             tanh(0, j)
@@ -329,7 +329,7 @@ def tile_oddlayer_t_kernel(
 
         banks = [(s, b) for s in range(3, PAIRS) for b in range(3)]
         passes = [(r, j, g) for r in range(2, PAIRS) for j in range(2) for g in range(3)]
-        passes = passes[:-3]
+        passes = passes[:-6]
         first = True
         while passes:
             n = FIRST_BANKS if first else RUN_BANKS
@@ -352,9 +352,11 @@ def tile_oddlayer_t_kernel(
                 one_pass(r, j, g)
                 if g == 2:
                     tanh(r, j)
+                    flush()
                     if r >= 13:
                         clip(r, j, j + 1)
                         store(2 * r + j, 1)
                     elif j == 1:
                         pending.append(r)
-        last_tile()
+        for j in range(2):
+            by_halves(PAIRS - 1, j)

@@ -24,9 +24,9 @@ LOADS = (
     + [(k, t, 4) for t in range(16, TILES, 4) for k in ("x", "l")]
 )
 VC = [320, 256, 288]
-RUN_BANKS = 4
-RUN_PASSES = 8
-FIRST_BANKS = 5
+RUN_BANKS = 3
+RUN_PASSES = 6
+FIRST_BANKS = 6
 
 
 def tile_oddlayer_t_kernel(

@@ -26,7 +26,7 @@ LOADS = (
 VC = [320, 256, 288]
 RUN_BANKS = 3
 RUN_PASSES = 6
-FIRST_BANKS = 6
+EXTRA_BANKS = 2
 
 
 def tile_oddlayer_t_kernel(
@@ -64,11 +64,11 @@ def tile_oddlayer_t_kernel(
                 g = load[1]
                 wt = wpool.tile([P, 2048], BF16, name="wr%d" % g)
                 mt = wpool.tile([P, 2048], BF16, name="mr%d" % g)
-                for u in range(2):
+                for us in ((0, 1), (1, 2)) if g == 0 else ((0, 2),):
                     for dst, src in ((wt, w_src[g]), (mt, m_src[g])):
                         nc.sync.dma_start(
-                            out=dst[:, 1024 * u : 1024 * u + 1024],
-                            in_=src[256 * u : 256 * u + 256, :].rearrange("(p e) c -> p (e c)", e=2),
+                            out=dst[:, 1024 * us[0] : 1024 * us[1]].rearrange("p (u f) -> p u f", f=1024),
+                            in_=src[256 * us[0] : 256 * us[1], :].rearrange("(u p e) c -> p u (e c)", p=P, e=2),
                         )
                 wr[g] = wt
                 mr[g] = mt
@@ -92,10 +92,10 @@ def tile_oddlayer_t_kernel(
             wgt = wpool.tile([P, 2048], BF16, name="wg%d" % g, align_bytes=64)
             wg.append(wgt)
 
-        def w_mask(g, u):
-            half = slice(1024 * u, 1024 * u + 1024)
-            w3 = wr[g][:, half].rearrange("p (e c) -> p e c", e=2)[:, :, VC[g] : 512]
-            m3 = mr[g][:, half].rearrange("p (e c) -> p e c", e=2)[:, :, VC[g] : 512]
+        def w_mask(g, u0, u1):
+            part = slice(1024 * u0, 1024 * u1)
+            w3 = wr[g][:, part].rearrange("p (t c) -> p t c", c=512)[:, :, VC[g] : 512]
+            m3 = mr[g][:, part].rearrange("p (t c) -> p t c", c=512)[:, :, VC[g] : 512]
             nc.vector.tensor_tensor(out=w3, in0=w3, in1=m3, op=ALU.mult)
 
         def w_regroup_s(g):
@@ -274,40 +274,39 @@ def tile_oddlayer_t_kernel(
                 d0 = (2 * r + j) * 512 + 256 * h
                 nc.sync.dma_start(out=o_view[:, d0 : d0 + 256], in_=seg)
 
-        w_mask(0, 0)
-        w_mask(0, 1)
+        w_mask(0, 0, 1)
+        w_mask(0, 1, 2)
         w_regroup_s(0)
         w_fused_v(0)
         dummy(3, 0, 0)
         t_bank(0, 0, "s")
-        dummy(1, 0, 0)
+        dummy(2, 0, 0)
         t_bank(1, 0, "s")
         t_bank(2, 0, "s")
         dummy(1, 0, 0)
         w_quant(0)
         q_x(0)
-        w_mask(1, 0)
         q_x(1)
         for r in range(2):
             for j in range(2):
                 one_pass(r, j, 0)
-        dummy(1, 0, 0)
-        w_mask(1, 1)
+        dummy(2, 0, 0)
+        w_mask(1, 0, 2)
         w_regroup_s(1)
         w_fused_v(1)
         t_bank(0, 1, "s")
         t_bank(0, 2, "s")
         q_x(2)
         w_quant(1)
-        w_mask(2, 0)
         q_l(0, 0, 1)
         q_l(0, 1, 2)
-        w_mask(2, 1)
+        w_mask(2, 0, 2)
         w_regroup_s(2)
         w_fused_v(2)
-        dummy(8, 0, 0)
+        dummy(5, 0, 0)
         one_pass(0, 0, 1)
         one_pass(0, 1, 1)
+        dummy(3, 0, 0)
         t_bank(1, 1, "s")
         t_bank(1, 2, "s")
         w_quant(2)
@@ -330,10 +329,10 @@ def tile_oddlayer_t_kernel(
         banks = [(s, b) for s in range(3, PAIRS) for b in range(3)]
         passes = [(r, j, g) for r in range(2, PAIRS) for j in range(2) for g in range(3)]
         passes = passes[:-6]
-        first = True
+        extra = EXTRA_BANKS
         while passes:
-            n = FIRST_BANKS if first else RUN_BANKS
-            first = False
+            n = RUN_BANKS + min(1, extra)
+            extra -= min(1, extra)
             run = banks[:n]
             banks = banks[n:]
             for i, (s, b) in enumerate(run):

@@ -26,7 +26,8 @@ LOADS = (
 VC = [320, 256, 288]
 RUN_BANKS = 3
 RUN_PASSES = 6
-EXTRA_BANKS = 2
+FIRST_PASSES = 4
+SHORT_RUNS = 6
 
 
 def tile_oddlayer_t_kernel(
@@ -39,7 +40,7 @@ def tile_oddlayer_t_kernel(
         acts = ctx.enter_context(tc.tile_pool(name="acts", bufs=1))
         wpool = ctx.enter_context(tc.tile_pool(name="wpool", bufs=1))
         gpool = ctx.enter_context(tc.tile_pool(name="gpool", bufs=3))
-        cpool = ctx.enter_context(tc.tile_pool(name="cpool", bufs=5))
+        cpool = ctx.enter_context(tc.tile_pool(name="cpool", bufs=6))
         opool = ctx.enter_context(tc.tile_pool(name="opool", bufs=6))
         psum = ctx.enter_context(tc.psum_pool(name="psum", bufs=1))
 
@@ -329,12 +330,10 @@ def tile_oddlayer_t_kernel(
         banks = [(s, b) for s in range(3, PAIRS) for b in range(3)]
         passes = [(r, j, g) for r in range(2, PAIRS) for j in range(2) for g in range(3)]
         passes = passes[:-6]
-        extra = EXTRA_BANKS
+        short = SHORT_RUNS
         while passes:
-            n = RUN_BANKS + min(1, extra)
-            extra -= min(1, extra)
-            run = banks[:n]
-            banks = banks[n:]
+            run = banks[:RUN_BANKS]
+            banks = banks[RUN_BANKS:]
             for i, (s, b) in enumerate(run):
                 t_bank(s, b, "v" if b == 0 else "s")
                 if i == 0:
@@ -345,8 +344,10 @@ def tile_oddlayer_t_kernel(
                     q_l(s, 0, 2)
             if not run:
                 flush()
-            part = passes[:RUN_PASSES]
-            passes = passes[RUN_PASSES:]
+            n = FIRST_PASSES if short else RUN_PASSES
+            short -= min(1, short)
+            part = passes[:n]
+            passes = passes[n:]
             for (r, j, g) in part:
                 one_pass(r, j, g)
                 if g == 2:

@@ -23,7 +23,7 @@ LOADS = (
     + [(k, t + i, n) for t in (8, 12) for (k, i, n) in (("x", 0, 4), ("l", 0, 2), ("l", 2, 2))]
     + [(k, t, 4) for t in range(16, TILES, 4) for k in ("x", "l")]
 )
-VC = [320, 256, 288]
+VB = [64, 64, 64]
 RUN_BANKS = 3
 RUN_PASSES = 6
 FIRST_PASSES = 4
@@ -93,24 +93,18 @@ def tile_oddlayer_t_kernel(
             wgt = wpool.tile([P, 2048], BF16, name="wg%d" % g, align_bytes=64)
             wg.append(wgt)
 
-        def w_mask(g, u0, u1):
+        def w_mask(g, u0, u1, columns):
             part = slice(1024 * u0, 1024 * u1)
-            w3 = wr[g][:, part].rearrange("p (t c) -> p t c", c=512)[:, :, VC[g] : 512]
-            m3 = mr[g][:, part].rearrange("p (t c) -> p t c", c=512)[:, :, VC[g] : 512]
+            cols = slice(4 * VB[g], 512) if columns == "s" else slice(0, 4 * VB[g])
+            w3 = wr[g][:, part].rearrange("p (t c) -> p t c", c=512)[:, :, cols]
+            m3 = mr[g][:, part].rearrange("p (t c) -> p t c", c=512)[:, :, cols]
             nc.vector.tensor_tensor(out=w3, in0=w3, in1=m3, op=ALU.mult)
 
-        def w_regroup_s(g):
+        def w_regroup(g):
             src = wr[g][:].rearrange("p (t c i) -> p c t i", t=4, i=4)
             dst = wg[g][:].rearrange("p (c i t) -> p c t i", i=4, t=4)
-            nc.scalar.copy(out=dst[:, VC[g] // 4 : 128], in_=src[:, VC[g] // 4 : 128])
-
-        def w_fused_v(g):
-            nc.vector.tensor_tensor(
-                out=wg[g][:, 0 : 4 * VC[g]].rearrange("p (c t) -> p c t", t=4),
-                in0=wr[g][:].rearrange("p (t c) -> p c t", t=4)[:, 0 : VC[g]],
-                in1=mr[g][:].rearrange("p (t c) -> p c t", t=4)[:, 0 : VC[g]],
-                op=ALU.mult,
-            )
+            nc.vector.tensor_copy(out=dst[:, 0 : VB[g]], in_=src[:, 0 : VB[g]])
+            nc.scalar.copy(out=dst[:, VB[g] : 128], in_=src[:, VB[g] : 128])
 
         def w_quant(g):
             nc.vector.quantize_mx(
@@ -275,10 +269,11 @@ def tile_oddlayer_t_kernel(
                 d0 = (2 * r + j) * 512 + 256 * h
                 nc.sync.dma_start(out=o_view[:, d0 : d0 + 256], in_=seg)
 
-        w_mask(0, 0, 1)
-        w_mask(0, 1, 2)
-        w_regroup_s(0)
-        w_fused_v(0)
+        w_mask(0, 0, 1, "s")
+        w_mask(0, 0, 1, "v")
+        w_mask(0, 1, 2, "s")
+        w_mask(0, 1, 2, "v")
+        w_regroup(0)
         dummy(3, 0, 0)
         t_bank(0, 0, "s")
         dummy(2, 0, 0)
@@ -292,18 +287,18 @@ def tile_oddlayer_t_kernel(
             for j in range(2):
                 one_pass(r, j, 0)
         dummy(2, 0, 0)
-        w_mask(1, 0, 2)
-        w_regroup_s(1)
-        w_fused_v(1)
+        w_mask(1, 0, 2, "s")
+        w_mask(1, 0, 2, "v")
+        w_regroup(1)
         t_bank(0, 1, "s")
         t_bank(0, 2, "s")
         q_x(2)
         w_quant(1)
         q_l(0, 0, 1)
         q_l(0, 1, 2)
-        w_mask(2, 0, 2)
-        w_regroup_s(2)
-        w_fused_v(2)
+        w_mask(2, 0, 2, "s")
+        w_mask(2, 0, 2, "v")
+        w_regroup(2)
         dummy(5, 0, 0)
         one_pass(0, 0, 1)
         one_pass(0, 1, 1)

@@ -274,12 +274,11 @@ def tile_oddlayer_t_kernel(
         w_mask(0, 1, 2, "s")
         w_mask(0, 1, 2, "v")
         w_regroup(0)
-        dummy(3, 0, 0)
+        dummy(4, 0, 0)
         t_bank(0, 0, "s")
         dummy(2, 0, 0)
         t_bank(1, 0, "s")
         t_bank(2, 0, "s")
-        dummy(1, 0, 0)
         w_quant(0)
         q_x(0)
         q_x(1)
@@ -306,6 +305,7 @@ def tile_oddlayer_t_kernel(
         t_bank(1, 1, "s")
         t_bank(1, 2, "s")
         w_quant(2)
+        dummy(1, 0, 0)
         t_bank(2, 1, "s")
         t_bank(2, 2, "s")
         q_l(1, 0, 1)

from contextlib import ExitStack

import concourse.mybir as mybir
from concourse.masks import make_identity

F32 = mybir.dt.float32
BF16 = mybir.dt.bfloat16
U32 = mybir.dt.uint32
U8 = mybir.dt.uint8
FP8X4 = mybir.dt.float8_e4m3fn_x4
ALU = mybir.AluOpType
ACT = mybir.ActivationFunctionType

P = 128
B, E, N = 4096, 512, 1024
TILES = B // P
PAIRS = TILES // 2
FLOPS = 2 * B * (E + N) * E
TANH5 = 0.9999092042625951

LOADS = (
    [("w", 0), ("x", 0, 2), ("x", 2, 4), ("w", 1), ("l", 0, 2), ("w", 2), ("l", 2, 2), ("l", 4, 2), ("x", 6, 2), ("l", 6, 2)]
    + [(k, t + i, n) for t in (8, 12) for (k, i, n) in (("x", 0, 4), ("l", 0, 2), ("l", 2, 2))]
    + [(k, t, 4) for t in range(16, TILES, 4) for k in ("x", "l")]
)
VB = [64, 64, 64]
RUN_BANKS = 3
RUN_PASSES = 6
FIRST_PASSES = 4
SHORT_RUNS = 6


def tile_oddlayer_t_kernel(
    tc, x, llr, odd_weights, llr_weights, w_odd2even_mask, w_skipconn2even_mask, out
):
    nc = tc.nc
    with ExitStack() as ctx:
        ctx.enter_context(tc.manual_schedule())
        const = ctx.enter_context(tc.tile_pool(name="const", bufs=1))
        acts = ctx.enter_context(tc.tile_pool(name="acts", bufs=1))
        wpool = ctx.enter_context(tc.tile_pool(name="wpool", bufs=1))
        gpool = ctx.enter_context(tc.tile_pool(name="gpool", bufs=3))
        cpool = ctx.enter_context(tc.tile_pool(name="cpool", bufs=6))
        opool = ctx.enter_context(tc.tile_pool(name="opool", bufs=6))
        psum = ctx.enter_context(tc.psum_pool(name="psum", bufs=1))

        ident = const.tile([P, P], F32)
        make_identity(nc, ident[:])
        warm_in = const.tile([P, 1], F32)
        warm_out = const.tile([P, 1], F32)
        nc.vector.memset(warm_in[:], 0.0)
        nc.scalar.activation(out=warm_out[:], in_=warm_in[:], func=ACT.Tanh, scale=0.5)

        w_src = [odd_weights, llr_weights[0:512, :], llr_weights[512:1024, :]]
        m_src = [w_odd2even_mask, w_skipconn2even_mask[0:512, :], w_skipconn2even_mask[512:1024, :]]
        x_view = x.rearrange("(p t) k -> p (t k)", t=TILES)
        l_view = llr.rearrange("(p t) k -> p (t k)", t=TILES)
        o_view = out.rearrange("(p t) e -> p (t e)", t=TILES)
        wr = {}
        mr = {}
        where_x = {}
        where_l = {}
        for load in LOADS:
            if load[0] == "w":
                g = load[1]
                wt = wpool.tile([P, 2048], BF16, name="wr%d" % g)
                mt = wpool.tile([P, 2048], BF16, name="mr%d" % g)
                for us in ((0, 1), (1, 2)) if g == 0 else ((0, 2),):
                    for dst, src in ((wt, w_src[g]), (mt, m_src[g])):
                        nc.sync.dma_start(
                            out=dst[:, 1024 * us[0] : 1024 * us[1]].rearrange("p (u f) -> p u f", f=1024),
                            in_=src[256 * us[0] : 256 * us[1], :].rearrange("(u p e) c -> p u (e c)", p=P, e=2),
                        )
                wr[g] = wt
                mr[g] = mt
            elif load[0] == "x":
                t0, n = load[1], load[2]
                xs = acts.tile([P, n * E], BF16, name="xs%d" % t0)
                nc.sync.dma_start(out=xs[:], in_=x_view[:, t0 * E : (t0 + n) * E])
                for i in range(n):
                    where_x[t0 + i] = (xs, i)
            else:
                t0, n = load[1], load[2]
                ls = acts.tile([P, n * N], BF16, name="ls%d" % t0)
                nc.sync.dma_start(out=ls[:], in_=l_view[:, t0 * N : (t0 + n) * N])
                for i in range(n):
                    where_l[t0 + i] = (ls, i)

        wc = wpool.tile([P, 3 * 512], U32, align_bytes=64)
        ws = wpool.tile([P, 3 * 512], U8, align_bytes=64)
        wg = []
        for g in range(3):
            wgt = wpool.tile([P, 2048], BF16, name="wg%d" % g, align_bytes=64)
            wg.append(wgt)

        def w_mask(g, u0, u1, columns):
            part = slice(1024 * u0, 1024 * u1)
            cols = slice(4 * VB[g], 512) if columns == "s" else slice(0, 4 * VB[g])
            w3 = wr[g][:, part].rearrange("p (t c) -> p t c", c=512)[:, :, cols]
            m3 = mr[g][:, part].rearrange("p (t c) -> p t c", c=512)[:, :, cols]
            nc.vector.tensor_tensor(out=w3, in0=w3, in1=m3, op=ALU.mult)

        def w_regroup(g):
            src = wr[g][:].rearrange("p (t c i) -> p c t i", t=4, i=4)
            dst = wg[g][:].rearrange("p (c i t) -> p c t i", i=4, t=4)
            nc.vector.tensor_copy(out=dst[:, 0 : VB[g]], in_=src[:, 0 : VB[g]])
            nc.scalar.copy(out=dst[:, VB[g] : 128], in_=src[:, VB[g] : 128])

        def w_quant(g):
            nc.vector.quantize_mx(
                out=wc[:, 512 * g : 512 * g + 512].bitcast(FP8X4),
                scales=ws[:, 512 * g : 512 * g + 512],
                in_=wg[g][:],
            )

        free = list(range(8))

        def take():
            k = free[0]
            free.remove(k)
            return k

        grouped = {}
        codes = {}
        obuf = {}
        accs = {}

        def t_bank(s, b, engine):
            if b == 0:
                gx = gpool.tile([P, 1024], BF16, align_bytes=64)
                gl = gpool.tile([P, 2048], BF16, align_bytes=64)
                grouped[s] = (gx, gl)
            gx, gl = grouped[s]
            k = take()
            tp = psum.tile([P, 512], F32, tag="bank%d" % k)
            for a in range(2):
                for u in range(2):
                    if b == 0:
                        xs, i = where_x[2 * s + a]
                        src = xs[:].bitcast(F32)[:, i * 256 + 128 * u : i * 256 + 128 * u + 128]
                    else:
                        ls, i = where_l[2 * s + b - 1]
                        c0 = i * 512 + 256 * a + 128 * u
                        src = ls[:].bitcast(F32)[:, c0 : c0 + 128]
                    q = 2 * a + u
                    nc.tensor.transpose(tp[:, 128 * q : 128 * q + 128], src, ident[:])
            if b == 0:
                dst = gx[:].bitcast(F32)
            else:
                dst = gl[:].bitcast(F32)[:, 512 * (b - 1) : 512 * b]
            dst = dst.rearrange("p (a r u) -> p a r u", a=2, u=2)
            srcv = tp[:].rearrange("p (a u r) -> p a r u", a=2, u=2)
            if engine == "v":
                nc.vector.tensor_copy(out=dst, in_=srcv)
            else:
                nc.scalar.copy(out=dst, in_=srcv)
            free.append(k)

        def q_x(s):
            gx, gl = grouped[s]
            cx = cpool.tile([P, 256], U32, align_bytes=64)
            sx = cpool.tile([P, 256], U8, align_bytes=64)
            cl = cpool.tile([P, 512], U32, align_bytes=64)
            sl = cpool.tile([P, 512], U8, align_bytes=64)
            codes[s] = (cx, sx, cl, sl)
            nc.vector.quantize_mx(out=cx[:].bitcast(FP8X4), scales=sx[:], in_=gx[:])

        def q_l(s, j0, j1):
            gx, gl = grouped[s]
            cx, sx, cl, sl = codes[s]
            nc.vector.quantize_mx(
                out=cl[:, 256 * j0 : 256 * j1].bitcast(FP8X4),
                scales=sl[:, 256 * j0 : 256 * j1],
                in_=gl[:, 1024 * j0 : 1024 * j1],
            )

        def one_pass(r, j, g):
            if g == 0:
                k = take()
                acc = psum.tile([P, 512], F32, tag="bank%d" % k)
                accs[(r, j)] = (acc, k)
            acc, k = accs[(r, j)]
            cx, sx, cl, sl = codes[r]
            if g == 0:
                cc, ss, c0 = cx, sx, 128 * j
            else:
                cc, ss, c0 = cl, sl, 256 * j + 128 * (g - 1)
            nc.tensor.matmul_mx(
                out=acc[:],
                lhsT=cc[:, c0 : c0 + 128].bitcast(FP8X4),
                lhsT_scale=ss[:, c0 : c0 + 128],
                rhs=wc[:, 512 * g : 512 * g + 512].bitcast(FP8X4),
                rhs_scale=ws[:, 512 * g : 512 * g + 512],
                start=(g == 0),
                stop=(g == 2),
            )

        def tanh(r, j):
            if r % 2 == 0 and j == 0:
                ob = opool.tile([P, 2048], F32)
                obuf[r // 2] = ob
            ob = obuf[r // 2]
            c0 = ((2 * r) % 4 + j) * 512
            acc, k = accs[(r, j)]
            nc.scalar.activation(out=ob[:, c0 : c0 + 512], in_=acc[:], func=ACT.Tanh, scale=0.5)
            free.append(k)

        def clip(r, j0, j1):
            ob = obuf[r // 2]
            c0 = ((2 * r) % 4 + j0) * 512
            c1 = ((2 * r) % 4 + j1) * 512
            nc.vector.tensor_scalar(
                out=ob[:, c0:c1], in0=ob[:, c0:c1], scalar1=TANH5, scalar2=-TANH5,
                op0=ALU.min, op1=ALU.max,
            )

        def store(t0, n):
            ob = obuf[t0 // 4]
            c0 = (t0 % 4) * 512
            nc.sync.dma_start(out=o_view[:, t0 * 512 : (t0 + n) * 512], in_=ob[:, c0 : c0 + n * 512])

        pending = []

        def flush():
            for r in pending:
                clip(r, 0, 2)
                if r >= 10:
                    store(2 * r, 2)
                elif r % 2 == 1:
                    store(2 * r - 2, 4)
            pending.clear()

        def dummy(n, g, u):
            c0 = 1024 * u
            junk = psum.tile([P, 512], F32, tag="bank%d" % free[1])
            for i in range(n):
                nc.tensor.matmul(
                    out=junk[:], lhsT=mr[g][:, c0 : c0 + 128], rhs=mr[g][:, c0 : c0 + 512],
                    start=(i == 0), stop=(i == n - 1),
                )

        def by_halves(r, j):
            cx, sx, cl, sl = codes[r]
            ob = obuf[r // 2]
            for h in range(2):
                k = take()
                half = psum.tile([P, 256], F32, tag="bank%d" % k)
                for g in range(3):
                    if g == 0:
                        cc, ss, c0 = cx, sx, 128 * j
                    else:
                        cc, ss, c0 = cl, sl, 256 * j + 128 * (g - 1)
                    w0 = 512 * g + 256 * h
                    nc.tensor.matmul_mx(
                        out=half[:],
                        lhsT=cc[:, c0 : c0 + 128].bitcast(FP8X4),
                        lhsT_scale=ss[:, c0 : c0 + 128],
                        rhs=wc[:, w0 : w0 + 256].bitcast(FP8X4),
                        rhs_scale=ws[:, w0 : w0 + 256],
                        start=(g == 0),
                        stop=(g == 2),
                    )
                o0 = ((2 * r) % 4 + j) * 512 + 256 * h
                seg = ob[:, o0 : o0 + 256]
                nc.scalar.activation(out=seg, in_=half[:], func=ACT.Tanh, scale=0.5)
                nc.vector.tensor_scalar(
                    out=seg, in0=seg, scalar1=TANH5, scalar2=-TANH5, op0=ALU.min, op1=ALU.max
                )
                d0 = (2 * r + j) * 512 + 256 * h
                nc.sync.dma_start(out=o_view[:, d0 : d0 + 256], in_=seg)

        w_mask(0, 0, 1, "s")
        w_mask(0, 0, 1, "v")
        w_mask(0, 1, 2, "s")
        w_mask(0, 1, 2, "v")
        w_regroup(0)
        dummy(4, 0, 0)
        t_bank(0, 0, "s")
        dummy(2, 0, 0)
        t_bank(1, 0, "s")
        t_bank(2, 0, "s")
        w_quant(0)
        q_x(0)
        q_x(1)
        for r in range(2):
            for j in range(2):
                one_pass(r, j, 0)
        dummy(2, 0, 0)
        w_mask(1, 0, 2, "s")
        w_mask(1, 0, 2, "v")
        w_regroup(1)
        t_bank(0, 1, "s")
        t_bank(0, 2, "s")
        q_x(2)
        w_quant(1)
        q_l(0, 0, 1)
        q_l(0, 1, 2)
        w_mask(2, 0, 2, "s")
        w_mask(2, 0, 2, "v")
        w_regroup(2)
        dummy(5, 0, 0)
        one_pass(0, 0, 1)
        one_pass(0, 1, 1)
        dummy(3, 0, 0)
        t_bank(1, 1, "s")
        t_bank(1, 2, "s")
        w_quant(2)
        dummy(1, 0, 0)
        t_bank(2, 1, "s")
        t_bank(2, 2, "s")
        q_l(1, 0, 1)
        q_l(1, 1, 2)
        for j in range(2):
            one_pass(0, j, 2)
            tanh(0, j)
        q_l(2, 0, 1)
        for j in range(2):
            one_pass(1, j, 1)
            one_pass(1, j, 2)
            tanh(1, j)
        q_l(2, 1, 2)
        pending.extend([0, 1])


        banks = [(s, b) for s in range(3, PAIRS) for b in range(3)]
        passes = [(r, j, g) for r in range(2, PAIRS) for j in range(2) for g in range(3)]
        passes = passes[:-6]
        short = SHORT_RUNS
        while passes:
            run = banks[:RUN_BANKS]
            banks = banks[RUN_BANKS:]
            for i, (s, b) in enumerate(run):
                t_bank(s, b, "v" if b == 0 else "s")
                if i == 0:
                    flush()
                if b == 1:
                    q_x(s)
                if b == 2:
                    q_l(s, 0, 2)
            if not run:
                flush()
            n = FIRST_PASSES if short else RUN_PASSES
            short -= min(1, short)
            part = passes[:n]
            passes = passes[n:]
            for (r, j, g) in part:
                one_pass(r, j, g)
                if g == 2:
                    tanh(r, j)
                    flush()
                    if r >= 13:
                        clip(r, j, j + 1)
                        store(2 * r + j, 1)
                    elif j == 1:
                        pending.append(r)
        for j in range(2):
            by_halves(PAIRS - 1, j)
